import numpy as np
import ml_dtypes


def mxq(x, axis, fmt="e4m3"):
    dtype, down = {"e4m3": (ml_dtypes.float8_e4m3fn, 7), "e5m2": (ml_dtypes.float8_e5m2, 14)}[fmt]
    v = np.moveaxis(np.asarray(x, np.float32).astype(ml_dtypes.bfloat16).astype(np.float64), axis, -1)
    blocks = v.reshape(v.shape[:-1] + (-1, 32))
    amax = np.abs(blocks).max(-1, keepdims=True)
    byte = np.maximum(np.where(amax > 0, np.frexp(amax)[1] - 1 + 127, 0) - down, 1)
    scale = np.exp2(byte - 127.0)
    codes = (blocks / scale).astype(np.float32).astype(dtype).astype(np.float64)
    return np.moveaxis((codes * scale).reshape(v.shape), -1, axis)


WIDE = False


def mx_kscale(k):
    if not WIDE:
        return np.ones(k)
    levels = np.array([10, -10, 5, -5, 0])
    a = np.random.permutation(np.resize(levels, k // 512 * 4)).reshape(k // 512, 4)
    idx = np.arange(k)
    return np.exp2(a[idx // 512, idx % 128 // 32])


BF16 = ml_dtypes.bfloat16


def bf(x):
    return np.asarray(x, np.float32).astype(BF16)


def f64(x):
    return np.asarray(x).astype(np.float64)


N, E, C, D1, D2 = 16384, 512, 128, 2, 2
T1 = D1 + 1


def shift_down(y, k):
    return np.pad(y, ((k, 0), (0, 0)))[:y.shape[0]] if k > 0 else y


def setup_inputs():
    s = mx_kscale(E)
    return {"x": bf(np.random.standard_normal((N, E)) * s),
            "W1": bf(np.random.standard_normal((T1, E, C)) * 0.4 / np.sqrt(E) / s[None, :, None]),
            "b1": bf(np.random.standard_normal((1, C)) * 0.25)}


def reference(x, W1, b1):
    Y = mxq(f64(x), 1, "e4m3") @ mxq(f64(W1), 1, "e4m3")
    S = sum(shift_down(Y[k], k) for k in range(T1))
    cnt1 = np.minimum(np.arange(N), D1) + 1.0
    return np.tanh(S + cnt1[:, None] * f64(b1)[0])

@@ -1,0 +1,201 @@
+from contextlib import ExitStack
+
+import concourse.mybir as mybir
+from concourse.masks import make_identity
+
+F32 = mybir.dt.float32
+BF16 = mybir.dt.bfloat16
+U32 = mybir.dt.uint32
+U8 = mybir.dt.uint8
+FP8X4 = mybir.dt.float8_e4m3fn_x4
+ADD = mybir.AluOpType.add
+TANH = mybir.ActivationFunctionType.Tanh
+
+P = 128
+N_ROWS = 16384
+E = 512
+C = 128
+TAPS = 3
+R = N_ROWS // P
+WORDS = E // 2
+FLOPS = 2 * N_ROWS * E * C * TAPS
+
+LEAD = 7
+UNITS = [(-2, 2), (0, 4), (4, 4)] + [(r, 8) for r in range(8, R, 8)]
+LOADS = [(R - 2, 2), (0, 4), (4, 4)] + [(r, 8) for r in range(8, R - 8, 8)] + [(R - 8, 6)]
+
+
+def tile_predictor_pa_t_kernel(tc, x, W1, b1, out):
+    nc = tc.nc
+    xv = x.rearrange("(j r) k -> j (r k)", r=R)
+    ov = out.rearrange("(j r) c -> j (r c)", r=R)
+    with ExitStack() as ctx:
+        const = ctx.enter_context(tc.tile_pool(name="const", bufs=1))
+        rawp = ctx.enter_context(tc.tile_pool(name="raw", bufs=1))
+        grp = ctx.enter_context(tc.tile_pool(name="grouped", bufs=3))
+        qp = ctx.enter_context(tc.tile_pool(name="quant", bufs=4))
+        outp = ctx.enter_context(tc.tile_pool(name="outs", bufs=6))
+        psum = ctx.enter_context(tc.psum_pool(name="psum", bufs=1))
+        ctx.enter_context(tc.manual_schedule())
+
+        raw_of = {}
+        blk = {}
+        state = {"a": 0, "b": 0, "load": 0}
+
+        def load_next():
+            if state["load"] >= len(LOADS):
+                return
+            r0, nb = LOADS[state["load"]]
+            state["load"] += 1
+            t = rawp.tile([P, nb * E], BF16, name="raw%d" % r0)
+            nc.sync.dma_start(out=t[:], in_=xv[:, r0 * E:(r0 + nb) * E])
+            for b in range(nb):
+                raw_of[r0 + b] = (t, b)
+
+        ident = const.tile([P, P], F32, name="ident")
+        make_identity(nc, ident[:])
+        warm = const.tile([P, 1], F32, name="warm")
+        nc.vector.memset(warm[:], 0.0)
+        nc.scalar.activation(out=warm[:], in_=warm[:], func=TANH)
+        bz = const.tile([P, C], BF16, name="bz")
+        nc.vector.memset(bz[:], 0.0)
+        nc.scalar.dma_start(out=bz[0:1, :], in_=b1)
+        coef = const.tile([P, TAPS, P], BF16, name="coef")
+        nc.vector.memset(coef[:], 3.0)
+        nc.vector.memset(coef[0:1, 0, 0:1], 1.0)
+        nc.vector.memset(coef[0:1, 1, 0:1], 2.0)
+        shift = const.tile([P, P], F32, name="shift")
+        nc.vector.memset(shift[:], 0.0)
+        nc.vector.tensor_copy(out=shift[:, 1:P], in_=ident[:, 0:P - 1])
+
+        load_next()
+        wraw = const.tile([P, TAPS, 4, C], BF16, name="wraw")
+        nc.sync.dma_start(
+            out=wraw[:].rearrange("p k (u e) c -> p k u (e c)", u=2),
+            in_=W1.rearrange("k (u p e) c -> p k u (e c)", u=2, p=P, e=2),
+        )
+        for i in range(LEAD):
+            load_next()
+
+        wg = const.tile([P, TAPS, C, 4], BF16, name="wg", align_bytes=64)
+        wq = const.tile([P, TAPS, C], U32, name="wq", align_bytes=64)
+        ws = const.tile([P, TAPS, C], U8, name="ws", align_bytes=64)
+        bias = const.tile([P, TAPS, C], F32, name="bias")
+
+        def prepare_w():
+            nc.vector.tensor_copy(out=wg[:], in_=wraw[:].rearrange("p k t c -> p k c t"))
+            for k in range(TAPS):
+                nc.vector.quantize_mx(
+                    out=wq[:, k, :].bitcast(FP8X4),
+                    scales=ws[:, k, :],
+                    in_=wg[:, k].rearrange("p c t -> p (c t)"),
+                )
+
+        def transposes(u):
+            r0, nb = UNITS[u]
+            banks = []
+            for h in range(nb // 2):
+                pa = psum.tile([P, 2, 2, P], F32, tag="a%d" % (state["a"] % 4), name="pa%d" % state["a"])
+                state["a"] += 1
+                for b in range(2):
+                    r = r0 + 2 * h + b
+                    t, i = raw_of[r % R]
+                    words = t[:].bitcast(F32)
+                    for v in range(2):
+                        lo = i * WORDS + v * P
+                        nc.tensor.transpose(pa[:, b, v, :], words[:, lo:lo + P], (shift if r < 0 else ident)[:])
+                banks.append(pa)
+            return banks
+
+        def leave_and_quantise(u, banks):
+            r0, nb = UNITS[u]
+            g = grp.tile([P, nb * 2 * P], F32, tag="g", name="g%d" % u, align_bytes=64)
+            for h, pa in enumerate(banks):
+                dst = g[:, h * 512:(h + 1) * 512].rearrange("p (b j v) -> p b j v", b=2, v=2)
+                src = pa[:].rearrange("p b v j -> p b j v")
+                if h == len(banks) - 1:
+                    nc.vector.tensor_copy(out=dst, in_=src)
+                else:
+                    nc.scalar.copy(out=dst, in_=src)
+            cq = qp.tile([P, nb * P], U32, tag="cq", name="cq%d" % u, align_bytes=64)
+            sq = qp.tile([P, nb * P], U8, tag="sq", name="sq%d" % u, align_bytes=64)
+            gb = g[:].bitcast(BF16)
+            step = min(nb * P, 512)
+            for a in range(0, nb * P, step):
+                nc.vector.quantize_mx(
+                    out=cq[:, a:a + step].bitcast(FP8X4),
+                    scales=sq[:, a:a + step],
+                    in_=gb[:, 4 * a:4 * (a + step)],
+                )
+            for b in range(nb):
+                blk[r0 + b] = (cq, sq, b)
+
+        def multiply(u):
+            r0, nb = UNITS[u]
+            banks = []
+            for q in range(0, nb, 4):
+                pb = psum.tile([P, 4, C], F32, tag="b%d" % (state["b"] % 4), name="pb%d" % state["b"])
+                state["b"] += 1
+                for bi in range(4):
+                    for k in range(TAPS):
+                        cq, sq, i = blk[r0 + q + bi - k]
+                        nc.tensor.matmul_mx(
+                            out=pb[:, bi, :],
+                            lhsT=cq[:, i * P:(i + 1) * P].bitcast(FP8X4),
+                            lhsT_scale=sq[:, i * P:(i + 1) * P],
+                            rhs=wq[:, k, :].bitcast(FP8X4),
+                            rhs_scale=ws[:, k, :],
+                            start=(k == 0),
+                            stop=(k == TAPS - 1),
+                        )
+                banks.append(pb)
+            return banks
+
+        def add_bias(u, o, q, pb):
+            r0, nb = UNITS[u]
+            ob = o[:, q * 512:(q + 1) * 512].rearrange("p (n c) -> p n c", c=C)
+            if r0 + 4 * q == 0:
+                nc.vector.tensor_tensor(out=ob[:, 0:3, :], in0=pb[:, 0:3, :], in1=bias[:], op=ADD)
+                nc.vector.tensor_tensor(out=ob[:, 3, :], in0=pb[:, 3, :], in1=bias[:, 2, :], op=ADD)
+            else:
+                nc.vector.tensor_tensor(
+                    out=ob, in0=pb[:], in1=bias[:, 2:3, :].to_broadcast([P, 4, C]), op=ADD
+                )
+
+        def tanh_store(u, o, lo, hi):
+            r0, nb = UNITS[u]
+            nc.scalar.activation(out=o[:, lo:hi], in_=o[:, lo:hi], func=TANH)
+            nc.sync.dma_start(out=ov[:, r0 * C + lo:r0 * C + hi], in_=o[:, lo:hi])
+
+        n_units = len(UNITS)
+        outs = {}
+        for p in range(n_units + 1):
+            if p < n_units:
+                banks = transposes(p)
+                if p == 1:
+                    pbias = psum.tile([P, TAPS, C], F32, tag="b3", name="pbias")
+                    for k in range(TAPS):
+                        nc.tensor.matmul(out=pbias[:, k, :], lhsT=coef[:, k, :], rhs=bz[:], start=True, stop=True)
+                leave_and_quantise(p, banks)
+                if p == 0:
+                    prepare_w()
+                if p == 1:
+                    nc.vector.tensor_copy(out=bias[:], in_=pbias[:])
+            last = p == n_units
+            if p >= 2:
+                u = p - 1
+                pbs = multiply(u)
+                o = outp.tile([P, UNITS[u][1] * C], F32, tag="o", name="o%d" % u)
+                outs[u] = o
+                if not last:
+                    for q, pb in enumerate(pbs):
+                        add_bias(u, o, q, pb)
+            if p >= 3:
+                u = p - 2
+                tanh_store(u, outs[u], 0, UNITS[u][1] * C)
+                load_next()
+            if last:
+                u = p - 1
+                for q, pb in enumerate(pbs):
+                    add_bias(u, outs[u], q, pb)
+                    tanh_store(u, outs[u], q * 512, (q + 1) * 512)

@@ -20,9 +20,10 @@ R = N_ROWS // P
 WORDS = E // 2
 FLOPS = 2 * N_ROWS * E * C * TAPS
 
-LEAD = 7
-UNITS = [(-2, 2), (0, 4), (4, 4)] + [(r, 8) for r in range(8, R, 8)]
+LEAD = 8
+UNITS = [(-2, 2), (0, 4), (4, 4), (8, 8)] + [(r, 16) for r in range(16, R, 16)]
 LOADS = [(R - 2, 2), (0, 4), (4, 4)] + [(r, 8) for r in range(8, R - 8, 8)] + [(R - 8, 6)]
+VECTOR_EXITS = {1: (), 2: (1,), 4: (3,), 8: (1, 3)}
 
 
 def tile_predictor_pa_t_kernel(tc, x, W1, b1, out):
@@ -31,10 +32,10 @@ def tile_predictor_pa_t_kernel(tc, x, W1, b1, out):
     ov = out.rearrange("(j r) c -> j (r c)", r=R)
     with ExitStack() as ctx:
         const = ctx.enter_context(tc.tile_pool(name="const", bufs=1))
-        rawp = ctx.enter_context(tc.tile_pool(name="raw", bufs=1))
-        grp = ctx.enter_context(tc.tile_pool(name="grouped", bufs=3))
-        qp = ctx.enter_context(tc.tile_pool(name="quant", bufs=4))
-        outp = ctx.enter_context(tc.tile_pool(name="outs", bufs=6))
+        rawp = ctx.enter_context(tc.tile_pool(name="raw", bufs=12))
+        grp = ctx.enter_context(tc.tile_pool(name="grouped", bufs=6))
+        qp = ctx.enter_context(tc.tile_pool(name="quant", bufs=12))
+        outp = ctx.enter_context(tc.tile_pool(name="outs", bufs=8))
         psum = ctx.enter_context(tc.psum_pool(name="psum", bufs=1))
         ctx.enter_context(tc.manual_schedule())
 
@@ -46,11 +47,19 @@ def tile_predictor_pa_t_kernel(tc, x, W1, b1, out):
             if state["load"] >= len(LOADS):
                 return
             r0, nb = LOADS[state["load"]]
+            if state["load"] == 0:
+                t = const.tile([P, nb * E], BF16, name="rawh")
+            else:
+                t = rawp.tile([P, nb * E], BF16, tag="raw", name="raw%d" % r0)
             state["load"] += 1
-            t = rawp.tile([P, nb * E], BF16, name="raw%d" % r0)
             nc.sync.dma_start(out=t[:], in_=xv[:, r0 * E:(r0 + nb) * E])
             for b in range(nb):
                 raw_of[r0 + b] = (t, b)
+
+        def psum_bank(kind):
+            t = psum.tile([P, 512], F32, tag="%s%d" % (kind, state[kind] % 4), name="p%s%d" % (kind, state[kind]))
+            state[kind] += 1
+            return t
 
         ident = const.tile([P, P], F32, name="ident")
         make_identity(nc, ident[:])
@@ -91,56 +100,59 @@ def tile_predictor_pa_t_kernel(tc, x, W1, b1, out):
                     in_=wg[:, k].rearrange("p c t -> p (c t)"),
                 )
 
-        def transposes(u):
+        def transpose_and_leave(u):
+            r0, nb = UNITS[u]
+            fills = nb // 2
+            gs = []
+            for first in range(0, fills, 4):
+                group = list(range(first, min(first + 4, fills)))
+                pas = {}
+                for h in group:
+                    pa = psum_bank("a")
+                    pas[h] = pa
+                    for b in range(2):
+                        r = r0 + 2 * h + b
+                        t, i = raw_of[r % R]
+                        words = t[:].bitcast(F32)
+                        for v in range(2):
+                            lo = i * WORDS + v * P
+                            nc.tensor.transpose(
+                                pa[:, (2 * b + v) * P:(2 * b + v + 1) * P],
+                                words[:, lo:lo + P],
+                                (shift if r < 0 else ident)[:],
+                            )
+                for h in group:
+                    if h % 2 == 0:
+                        g = grp.tile([P, min(nb, 4) * 2 * P], F32, tag="g", name="g%d_%d" % (u, h), align_bytes=64)
+                        gs.append(g)
+                    dst = gs[-1][:, (h % 2) * 512:(h % 2 + 1) * 512].rearrange("p (b j v) -> p b j v", b=2, v=2)
+                    src = pas[h][:].rearrange("p (b v j) -> p b j v", b=2, v=2)
+                    if h in VECTOR_EXITS[fills]:
+                        nc.vector.tensor_copy(out=dst, in_=src)
+                    else:
+                        nc.scalar.copy(out=dst, in_=src)
+            return gs
+
+        def quantise(u, n, g):
+            r0, nb = UNITS[u]
+            w = min(nb, 4)
+            cq = qp.tile([P, w * P], U32, tag="cq", name="cq%d_%d" % (u, n), align_bytes=64)
+            sq = qp.tile([P, w * P], U8, tag="sq", name="sq%d_%d" % (u, n), align_bytes=64)
+            nc.vector.quantize_mx(out=cq[:].bitcast(FP8X4), scales=sq[:], in_=g[:].bitcast(BF16))
+            for b in range(w):
+                blk[r0 + 4 * n + b] = (cq, sq, b)
+
+        def multiply(u, sizes):
             r0, nb = UNITS[u]
             banks = []
-            for h in range(nb // 2):
-                pa = psum.tile([P, 2, 2, P], F32, tag="a%d" % (state["a"] % 4), name="pa%d" % state["a"])
-                state["a"] += 1
-                for b in range(2):
-                    r = r0 + 2 * h + b
-                    t, i = raw_of[r % R]
-                    words = t[:].bitcast(F32)
-                    for v in range(2):
-                        lo = i * WORDS + v * P
-                        nc.tensor.transpose(pa[:, b, v, :], words[:, lo:lo + P], (shift if r < 0 else ident)[:])
-                banks.append(pa)
-            return banks
-
-        def leave_and_quantise(u, banks):
-            r0, nb = UNITS[u]
-            g = grp.tile([P, nb * 2 * P], F32, tag="g", name="g%d" % u, align_bytes=64)
-            for h, pa in enumerate(banks):
-                dst = g[:, h * 512:(h + 1) * 512].rearrange("p (b j v) -> p b j v", b=2, v=2)
-                src = pa[:].rearrange("p b v j -> p b j v")
-                if h == len(banks) - 1:
-                    nc.vector.tensor_copy(out=dst, in_=src)
-                else:
-                    nc.scalar.copy(out=dst, in_=src)
-            cq = qp.tile([P, nb * P], U32, tag="cq", name="cq%d" % u, align_bytes=64)
-            sq = qp.tile([P, nb * P], U8, tag="sq", name="sq%d" % u, align_bytes=64)
-            gb = g[:].bitcast(BF16)
-            step = min(nb * P, 512)
-            for a in range(0, nb * P, step):
-                nc.vector.quantize_mx(
-                    out=cq[:, a:a + step].bitcast(FP8X4),
-                    scales=sq[:, a:a + step],
-                    in_=gb[:, 4 * a:4 * (a + step)],
-                )
-            for b in range(nb):
-                blk[r0 + b] = (cq, sq, b)
-
-        def multiply(u):
-            r0, nb = UNITS[u]
-            banks = []
-            for q in range(0, nb, 4):
-                pb = psum.tile([P, 4, C], F32, tag="b%d" % (state["b"] % 4), name="pb%d" % state["b"])
-                state["b"] += 1
-                for bi in range(4):
+            r = r0
+            for n, size in enumerate(sizes):
+                pb = psum_bank("b" if n < 4 else "a")
+                for bi in range(size):
                     for k in range(TAPS):
-                        cq, sq, i = blk[r0 + q + bi - k]
+                        cq, sq, i = blk[r + bi - k]
                         nc.tensor.matmul_mx(
-                            out=pb[:, bi, :],
+                            out=pb[:, bi * C:(bi + 1) * C],
                             lhsT=cq[:, i * P:(i + 1) * P].bitcast(FP8X4),
                             lhsT_scale=sq[:, i * P:(i + 1) * P],
                             rhs=wq[:, k, :].bitcast(FP8X4),
@@ -148,54 +160,69 @@ def tile_predictor_pa_t_kernel(tc, x, W1, b1, out):
                             start=(k == 0),
                             stop=(k == TAPS - 1),
                         )
-                banks.append(pb)
+                banks.append((pb, r, size))
+                r += size
             return banks
 
-        def add_bias(u, o, q, pb):
-            r0, nb = UNITS[u]
-            ob = o[:, q * 512:(q + 1) * 512].rearrange("p (n c) -> p n c", c=C)
-            if r0 + 4 * q == 0:
-                nc.vector.tensor_tensor(out=ob[:, 0:3, :], in0=pb[:, 0:3, :], in1=bias[:], op=ADD)
-                nc.vector.tensor_tensor(out=ob[:, 3, :], in0=pb[:, 3, :], in1=bias[:, 2, :], op=ADD)
-            else:
-                nc.vector.tensor_tensor(
-                    out=ob, in0=pb[:], in1=bias[:, 2:3, :].to_broadcast([P, 4, C]), op=ADD
-                )
+        o_of = {}
 
-        def tanh_store(u, o, lo, hi):
-            r0, nb = UNITS[u]
-            nc.scalar.activation(out=o[:, lo:hi], in_=o[:, lo:hi], func=TANH)
-            nc.sync.dma_start(out=ov[:, r0 * C + lo:r0 * C + hi], in_=o[:, lo:hi])
+        def add_bias(pb, r, size):
+            if r % 8 == 0 or r not in o_of:
+                o = outp.tile([P, 8 * C], F32, tag="o", name="o%d" % r)
+                for b in range(8):
+                    o_of[r + b] = (o, b)
+            o, b = o_of[r]
+            ob = o[:, b * C:(b + size) * C].rearrange("p (n c) -> p n c", c=C)
+            pv = pb[:, 0:size * C].rearrange("p (n c) -> p n c", c=C)
+            if r == 0:
+                nc.vector.tensor_tensor(out=ob[:, 0:3, :], in0=pv[:, 0:3, :], in1=bias[:], op=ADD)
+                nc.vector.tensor_tensor(out=ob[:, 3, :], in0=pv[:, 3, :], in1=bias[:, 2, :], op=ADD)
+            else:
+                nc.vector.tensor_tensor(out=ob, in0=pv, in1=bias[:, 2:3, :].to_broadcast([P, size, C]), op=ADD)
+
+        def tanh_store(r, size):
+            o, b = o_of[r]
+            nc.scalar.activation(out=o[:, b * C:(b + size) * C], in_=o[:, b * C:(b + size) * C], func=TANH)
+            nc.sync.dma_start(out=ov[:, r * C:(r + size) * C], in_=o[:, b * C:(b + size) * C])
 
         n_units = len(UNITS)
-        outs = {}
         for p in range(n_units + 1):
-            if p < n_units:
-                banks = transposes(p)
+            last = p == n_units
+            late = []
+            if not last:
+                gs = transpose_and_leave(p)
+                if p == 0:
+                    prepare_w()
                 if p == 1:
                     pbias = psum.tile([P, TAPS, C], F32, tag="b3", name="pbias")
                     for k in range(TAPS):
                         nc.tensor.matmul(out=pbias[:, k, :], lhsT=coef[:, k, :], rhs=bz[:], start=True, stop=True)
-                leave_and_quantise(p, banks)
-                if p == 0:
-                    prepare_w()
+                for n, g in enumerate(gs):
+                    if n == 3:
+                        late.append((n, g))
+                    else:
+                        quantise(p, n, g)
                 if p == 1:
                     nc.vector.tensor_copy(out=bias[:], in_=pbias[:])
-            last = p == n_units
+            banks = []
             if p >= 2:
-                u = p - 1
-                pbs = multiply(u)
-                o = outp.tile([P, UNITS[u][1] * C], F32, tag="o", name="o%d" % u)
-                outs[u] = o
-                if not last:
-                    for q, pb in enumerate(pbs):
-                        add_bias(u, o, q, pb)
+                nb = UNITS[p - 1][1]
+                banks = multiply(p - 1, [4, 4, 4, 2, 2] if last else [4] * (nb // 4))
+            if not last:
+                for n, (pb, r, size) in enumerate(banks):
+                    add_bias(pb, r, size)
+                    if n == 0:
+                        for m, g in late:
+                            quantise(p, m, g)
+                        late = []
+                for m, g in late:
+                    quantise(p, m, g)
             if p >= 3:
-                u = p - 2
-                tanh_store(u, outs[u], 0, UNITS[u][1] * C)
-                load_next()
+                r0, nb = UNITS[p - 2]
+                for r in range(r0, r0 + nb, 8):
+                    tanh_store(r, min(nb, 8))
+                    load_next()
             if last:
-                u = p - 1
-                for q, pb in enumerate(pbs):
-                    add_bias(u, outs[u], q, pb)
-                    tanh_store(u, outs[u], q * 512, (q + 1) * 512)
+                for pb, r, size in banks:
+                    add_bias(pb, r, size)
+                    tanh_store(r, size)

@@ -21,7 +21,7 @@ WORDS = E // 2
 FLOPS = 2 * N_ROWS * E * C * TAPS
 
 LEAD = 8
-UNITS = [(-2, 2), (0, 4), (4, 4), (8, 8)] + [(r, 16) for r in range(16, R, 16)]
+UNITS = [(-2, 2), (0, 4), (4, 4)] + [(r, 8) for r in range(8, R, 8)]
 LOADS = [(R - 2, 2), (0, 4), (4, 4)] + [(r, 8) for r in range(8, R - 8, 8)] + [(R - 8, 6)]
 VECTOR_EXITS = {1: (), 2: (1,), 4: (3,), 8: (1, 3)}
 
@@ -87,16 +87,16 @@ def tile_predictor_pa_t_kernel(tc, x, W1, b1, out):
             load_next()
 
         wg = const.tile([P, TAPS, C, 4], BF16, name="wg", align_bytes=64)
-        wq = const.tile([P, TAPS, C], U32, name="wq", align_bytes=64)
-        ws = const.tile([P, TAPS, C], U8, name="ws", align_bytes=64)
+        wq = const.tile([P, TAPS * C], U32, name="wq", align_bytes=64)
+        ws = const.tile([P, TAPS * C], U8, name="ws", align_bytes=64)
         bias = const.tile([P, TAPS, C], F32, name="bias")
 
         def prepare_w():
             nc.vector.tensor_copy(out=wg[:], in_=wraw[:].rearrange("p k t c -> p k c t"))
             for k in range(TAPS):
                 nc.vector.quantize_mx(
-                    out=wq[:, k, :].bitcast(FP8X4),
-                    scales=ws[:, k, :],
+                    out=wq[:, k * C:(k + 1) * C].bitcast(FP8X4),
+                    scales=ws[:, k * C:(k + 1) * C],
                     in_=wg[:, k].rearrange("p c t -> p (c t)"),
                 )
 
@@ -148,18 +148,21 @@ def tile_predictor_pa_t_kernel(tc, x, W1, b1, out):
             r = r0
             for n, size in enumerate(sizes):
                 pb = psum_bank("b" if n < 4 else "a")
-                for bi in range(size):
-                    for k in range(TAPS):
-                        cq, sq, i = blk[r + bi - k]
-                        nc.tensor.matmul_mx(
-                            out=pb[:, bi * C:(bi + 1) * C],
-                            lhsT=cq[:, i * P:(i + 1) * P].bitcast(FP8X4),
-                            lhsT_scale=sq[:, i * P:(i + 1) * P],
-                            rhs=wq[:, k, :].bitcast(FP8X4),
-                            rhs_scale=ws[:, k, :],
-                            start=(k == 0),
-                            stop=(k == TAPS - 1),
-                        )
+                passes = [(r + h, 0, 2, h) for h in range(0, size, 2)]
+                passes += [(r + h - 1, 1, 2, h) for h in range(0, size, 2)]
+                for h in range(0, size, 2):
+                    passes += [(r + h - 2, 2, 1, h), (r + h + 1, 0, 1, h + 1)]
+                for m, (s, k, nk, ob) in enumerate(passes):
+                    cq, sq, i = blk[s]
+                    nc.tensor.matmul_mx(
+                        out=pb[:, ob * C:(ob + nk) * C],
+                        lhsT=cq[:, i * P:(i + 1) * P].bitcast(FP8X4),
+                        lhsT_scale=sq[:, i * P:(i + 1) * P],
+                        rhs=wq[:, k * C:(k + nk) * C].bitcast(FP8X4),
+                        rhs_scale=ws[:, k * C:(k + nk) * C],
+                        start=(m == 0),
+                        stop=(m == len(passes) - 1),
+                    )
                 banks.append((pb, r, size))
                 r += size
             return banks
@@ -207,7 +210,7 @@ def tile_predictor_pa_t_kernel(tc, x, W1, b1, out):
             banks = []
             if p >= 2:
                 nb = UNITS[p - 1][1]
-                banks = multiply(p - 1, [4, 4, 4, 2, 2] if last else [4] * (nb // 4))
+                banks = multiply(p - 1, [4, 2, 2] if last else [4] * (nb // 4))
             if not last:
                 for n, (pb, r, size) in enumerate(banks):
                     add_bias(pb, r, size)
@@ -219,8 +222,9 @@ def tile_predictor_pa_t_kernel(tc, x, W1, b1, out):
                     quantise(p, m, g)
             if p >= 3:
                 r0, nb = UNITS[p - 2]
-                for r in range(r0, r0 + nb, 8):
-                    tanh_store(r, min(nb, 8))
+                piece = 4 if last else min(nb, 8)
+                for r in range(r0, r0 + nb, piece):
+                    tanh_store(r, piece)
                     load_next()
             if last:
                 for pb, r, size in banks:

@@ -20,7 +20,7 @@ R = N_ROWS // P
 WORDS = E // 2
 FLOPS = 2 * N_ROWS * E * C * TAPS
 
-LEAD = 8
+LEAD = 12
 UNITS = [(-2, 2), (0, 4), (4, 4)] + [(r, 8) for r in range(8, R, 8)]
 LOADS = [(R - 2, 2), (0, 4), (4, 4)] + [(r, 8) for r in range(8, R - 8, 8)] + [(R - 8, 6)]
 VECTOR_EXITS = {1: (), 2: (1,), 4: (3,), 8: (1, 3)}
@@ -41,7 +41,7 @@ def tile_predictor_pa_t_kernel(tc, x, W1, b1, out):
 
         raw_of = {}
         blk = {}
-        state = {"a": 0, "b": 0, "load": 0}
+        state = {"a": 0, "b": 0, "load": 0, "stored": 0}
 
         def load_next():
             if state["load"] >= len(LOADS):
@@ -100,6 +100,15 @@ def tile_predictor_pa_t_kernel(tc, x, W1, b1, out):
                     in_=wg[:, k].rearrange("p c t -> p (c t)"),
                 )
 
+        waiting = []
+
+        def flush_stores(keep):
+            while state["stored"] < len(waiting) - keep:
+                r, size = waiting[state["stored"]]
+                state["stored"] += 1
+                o, b = o_of[r]
+                nc.scalar.dma_start(out=ov[:, r * C:(r + size) * C], in_=o[:, b * C:(b + size) * C])
+
         def transpose_and_leave(u):
             r0, nb = UNITS[u]
             fills = nb // 2
@@ -131,6 +140,7 @@ def tile_predictor_pa_t_kernel(tc, x, W1, b1, out):
                         nc.vector.tensor_copy(out=dst, in_=src)
                     else:
                         nc.scalar.copy(out=dst, in_=src)
+                        flush_stores(0)
             return gs
 
         def quantise(u, n, g):
@@ -186,7 +196,7 @@ def tile_predictor_pa_t_kernel(tc, x, W1, b1, out):
         def tanh_store(r, size):
             o, b = o_of[r]
             nc.scalar.activation(out=o[:, b * C:(b + size) * C], in_=o[:, b * C:(b + size) * C], func=TANH)
-            nc.sync.dma_start(out=ov[:, r * C:(r + size) * C], in_=o[:, b * C:(b + size) * C])
+            waiting.append((r, size))
 
         n_units = len(UNITS)
         for p in range(n_units + 1):
@@ -194,6 +204,8 @@ def tile_predictor_pa_t_kernel(tc, x, W1, b1, out):
             late = []
             if not last:
                 gs = transpose_and_leave(p)
+                if p >= 1:
+                    load_next()
                 if p == 0:
                     prepare_w()
                 if p == 1:
@@ -225,8 +237,11 @@ def tile_predictor_pa_t_kernel(tc, x, W1, b1, out):
                 piece = 4 if last else min(nb, 8)
                 for r in range(r0, r0 + nb, piece):
                     tanh_store(r, piece)
-                    load_next()
+                    if last:
+                        flush_stores(1)
             if last:
                 for pb, r, size in banks:
                     add_bias(pb, r, size)
                     tanh_store(r, size)
+                    flush_stores(1)
+                flush_stores(0)

@@ -20,7 +20,7 @@ R = N_ROWS // P
 WORDS = E // 2
 FLOPS = 2 * N_ROWS * E * C * TAPS
 
-LEAD = 12
+LEAD = 17
 UNITS = [(-2, 2), (0, 4), (4, 4)] + [(r, 8) for r in range(8, R, 8)]
 LOADS = [(R - 2, 2), (0, 4), (4, 4)] + [(r, 8) for r in range(8, R - 8, 8)] + [(R - 8, 6)]
 VECTOR_EXITS = {1: (), 2: (1,), 4: (3,), 8: (1, 3)}
@@ -32,16 +32,16 @@ def tile_predictor_pa_t_kernel(tc, x, W1, b1, out):
     ov = out.rearrange("(j r) c -> j (r c)", r=R)
     with ExitStack() as ctx:
         const = ctx.enter_context(tc.tile_pool(name="const", bufs=1))
-        rawp = ctx.enter_context(tc.tile_pool(name="raw", bufs=12))
-        grp = ctx.enter_context(tc.tile_pool(name="grouped", bufs=6))
-        qp = ctx.enter_context(tc.tile_pool(name="quant", bufs=12))
-        outp = ctx.enter_context(tc.tile_pool(name="outs", bufs=8))
+        rawp = ctx.enter_context(tc.tile_pool(name="raw", bufs=1))
+        grp = ctx.enter_context(tc.tile_pool(name="grouped", bufs=4))
+        qp = ctx.enter_context(tc.tile_pool(name="quant", bufs=8))
+        outp = ctx.enter_context(tc.tile_pool(name="outs", bufs=12))
         psum = ctx.enter_context(tc.psum_pool(name="psum", bufs=1))
         ctx.enter_context(tc.manual_schedule())
 
         raw_of = {}
         blk = {}
-        state = {"a": 0, "b": 0, "load": 0, "stored": 0}
+        state = {"a": 0, "b": 0, "load": 0}
 
         def load_next():
             if state["load"] >= len(LOADS):
@@ -50,7 +50,7 @@ def tile_predictor_pa_t_kernel(tc, x, W1, b1, out):
             if state["load"] == 0:
                 t = const.tile([P, nb * E], BF16, name="rawh")
             else:
-                t = rawp.tile([P, nb * E], BF16, tag="raw", name="raw%d" % r0)
+                t = rawp.tile([P, nb * E], BF16, name="raw%d" % r0)
             state["load"] += 1
             nc.sync.dma_start(out=t[:], in_=xv[:, r0 * E:(r0 + nb) * E])
             for b in range(nb):
@@ -100,15 +100,6 @@ def tile_predictor_pa_t_kernel(tc, x, W1, b1, out):
                     in_=wg[:, k].rearrange("p c t -> p (c t)"),
                 )
 
-        waiting = []
-
-        def flush_stores(keep):
-            while state["stored"] < len(waiting) - keep:
-                r, size = waiting[state["stored"]]
-                state["stored"] += 1
-                o, b = o_of[r]
-                nc.scalar.dma_start(out=ov[:, r * C:(r + size) * C], in_=o[:, b * C:(b + size) * C])
-
         def transpose_and_leave(u):
             r0, nb = UNITS[u]
             fills = nb // 2
@@ -140,7 +131,6 @@ def tile_predictor_pa_t_kernel(tc, x, W1, b1, out):
                         nc.vector.tensor_copy(out=dst, in_=src)
                     else:
                         nc.scalar.copy(out=dst, in_=src)
-                        flush_stores(0)
             return gs
 
         def quantise(u, n, g):
@@ -196,7 +186,7 @@ def tile_predictor_pa_t_kernel(tc, x, W1, b1, out):
         def tanh_store(r, size):
             o, b = o_of[r]
             nc.scalar.activation(out=o[:, b * C:(b + size) * C], in_=o[:, b * C:(b + size) * C], func=TANH)
-            waiting.append((r, size))
+            nc.sync.dma_start(out=ov[:, r * C:(r + size) * C], in_=o[:, b * C:(b + size) * C])
 
         n_units = len(UNITS)
         for p in range(n_units + 1):
@@ -204,8 +194,6 @@ def tile_predictor_pa_t_kernel(tc, x, W1, b1, out):
             late = []
             if not last:
                 gs = transpose_and_leave(p)
-                if p >= 1:
-                    load_next()
                 if p == 0:
                     prepare_w()
                 if p == 1:
@@ -237,11 +225,8 @@ def tile_predictor_pa_t_kernel(tc, x, W1, b1, out):
                 piece = 4 if last else min(nb, 8)
                 for r in range(r0, r0 + nb, piece):
                     tanh_store(r, piece)
-                    if last:
-                        flush_stores(1)
+                    load_next()
             if last:
                 for pb, r, size in banks:
                     add_bias(pb, r, size)
                     tanh_store(r, size)
-                    flush_stores(1)
-                flush_stores(0)

@@ -63,12 +63,12 @@ def tile_predictor_pa_t_kernel(tc, x, W1, b1, out):
 
         ident = const.tile([P, P], F32, name="ident")
         make_identity(nc, ident[:])
-        warm = const.tile([P, 1], F32, name="warm")
-        nc.vector.memset(warm[:], 0.0)
-        nc.scalar.activation(out=warm[:], in_=warm[:], func=TANH)
         bz = const.tile([P, C], BF16, name="bz")
         nc.vector.memset(bz[:], 0.0)
         nc.scalar.dma_start(out=bz[0:1, :], in_=b1)
+        warm = const.tile([P, 1], F32, name="warm")
+        nc.vector.memset(warm[:], 0.0)
+        nc.scalar.activation(out=warm[:], in_=warm[:], func=TANH)
         coef = const.tile([P, TAPS, P], BF16, name="coef")
         nc.vector.memset(coef[:], 3.0)
         nc.vector.memset(coef[0:1, 0, 0:1], 1.0)
@@ -196,21 +196,20 @@ def tile_predictor_pa_t_kernel(tc, x, W1, b1, out):
                 gs = transpose_and_leave(p)
                 if p == 0:
                     prepare_w()
-                if p == 1:
-                    pbias = psum.tile([P, TAPS, C], F32, tag="b3", name="pbias")
-                    for k in range(TAPS):
-                        nc.tensor.matmul(out=pbias[:, k, :], lhsT=coef[:, k, :], rhs=bz[:], start=True, stop=True)
                 for n, g in enumerate(gs):
                     if n == 3:
                         late.append((n, g))
                     else:
                         quantise(p, n, g)
-                if p == 1:
-                    nc.vector.tensor_copy(out=bias[:], in_=pbias[:])
             banks = []
             if p >= 2:
                 nb = UNITS[p - 1][1]
                 banks = multiply(p - 1, [4, 2, 2] if last else [4] * (nb // 4))
+            if p == 2:
+                pbias = psum.tile([P, TAPS, C], F32, tag="b3", name="pbias")
+                for k in range(TAPS):
+                    nc.tensor.matmul(out=pbias[:, k, :], lhsT=coef[:, k, :], rhs=bz[:], start=True, stop=True)
+                nc.vector.tensor_copy(out=bias[:], in_=pbias[:])
             if not last:
                 for n, (pb, r, size) in enumerate(banks):
                     add_bias(pb, r, size)

@@ -21,7 +21,7 @@ WORDS = E // 2
 FLOPS = 2 * N_ROWS * E * C * TAPS
 
 LEAD = 17
-UNITS = [(-2, 2), (0, 4), (4, 4)] + [(r, 8) for r in range(8, R, 8)]
+UNITS = [(-2, 2), (0, 4), (4, 4), (8, 8)] + [(r, 16) for r in range(16, R, 16)]
 LOADS = [(R - 2, 2), (0, 4), (4, 4)] + [(r, 8) for r in range(8, R - 8, 8)] + [(R - 8, 6)]
 VECTOR_EXITS = {1: (), 2: (1,), 4: (3,), 8: (1, 3)}
 
@@ -63,12 +63,12 @@ def tile_predictor_pa_t_kernel(tc, x, W1, b1, out):
 
         ident = const.tile([P, P], F32, name="ident")
         make_identity(nc, ident[:])
-        bz = const.tile([P, C], BF16, name="bz")
-        nc.vector.memset(bz[:], 0.0)
-        nc.scalar.dma_start(out=bz[0:1, :], in_=b1)
         warm = const.tile([P, 1], F32, name="warm")
         nc.vector.memset(warm[:], 0.0)
         nc.scalar.activation(out=warm[:], in_=warm[:], func=TANH)
+        bz = const.tile([P, C], BF16, name="bz")
+        nc.vector.memset(bz[:], 0.0)
+        nc.scalar.dma_start(out=bz[0:1, :], in_=b1)
         coef = const.tile([P, TAPS, P], BF16, name="coef")
         nc.vector.memset(coef[:], 3.0)
         nc.vector.memset(coef[0:1, 0, 0:1], 1.0)
@@ -196,20 +196,21 @@ def tile_predictor_pa_t_kernel(tc, x, W1, b1, out):
                 gs = transpose_and_leave(p)
                 if p == 0:
                     prepare_w()
+                if p == 1:
+                    pbias = psum.tile([P, TAPS, C], F32, tag="b3", name="pbias")
+                    for k in range(TAPS):
+                        nc.tensor.matmul(out=pbias[:, k, :], lhsT=coef[:, k, :], rhs=bz[:], start=True, stop=True)
                 for n, g in enumerate(gs):
                     if n == 3:
                         late.append((n, g))
                     else:
                         quantise(p, n, g)
+                if p == 1:
+                    nc.vector.tensor_copy(out=bias[:], in_=pbias[:])
             banks = []
             if p >= 2:
                 nb = UNITS[p - 1][1]
-                banks = multiply(p - 1, [4, 2, 2] if last else [4] * (nb // 4))
-            if p == 2:
-                pbias = psum.tile([P, TAPS, C], F32, tag="b3", name="pbias")
-                for k in range(TAPS):
-                    nc.tensor.matmul(out=pbias[:, k, :], lhsT=coef[:, k, :], rhs=bz[:], start=True, stop=True)
-                nc.vector.tensor_copy(out=bias[:], in_=pbias[:])
+                banks = multiply(p - 1, [4, 4, 4, 2, 2] if last else [4] * (nb // 4))
             if not last:
                 for n, (pb, r, size) in enumerate(banks):
                     add_bias(pb, r, size)

from contextlib import ExitStack

import concourse.mybir as mybir
from concourse.masks import make_identity

F32 = mybir.dt.float32
BF16 = mybir.dt.bfloat16
U32 = mybir.dt.uint32
U8 = mybir.dt.uint8
FP8X4 = mybir.dt.float8_e4m3fn_x4
ADD = mybir.AluOpType.add
TANH = mybir.ActivationFunctionType.Tanh

P = 128
N_ROWS = 16384
E = 512
C = 128
TAPS = 3
R = N_ROWS // P
WORDS = E // 2
FLOPS = 2 * N_ROWS * E * C * TAPS

LEAD = 17
UNITS = [(-2, 2), (0, 4), (4, 4), (8, 8)] + [(r, 16) for r in range(16, R, 16)]
LOADS = [(R - 2, 2), (0, 4), (4, 4)] + [(r, 8) for r in range(8, R - 8, 8)] + [(R - 8, 6)]
VECTOR_EXITS = {1: (), 2: (1,), 4: (3,), 8: (1, 3)}


def tile_predictor_pa_t_kernel(tc, x, W1, b1, out):
    nc = tc.nc
    xv = x.rearrange("(j r) k -> j (r k)", r=R)
    ov = out.rearrange("(j r) c -> j (r c)", r=R)
    with ExitStack() as ctx:
        const = ctx.enter_context(tc.tile_pool(name="const", bufs=1))
        rawp = ctx.enter_context(tc.tile_pool(name="raw", bufs=1))
        grp = ctx.enter_context(tc.tile_pool(name="grouped", bufs=4))
        qp = ctx.enter_context(tc.tile_pool(name="quant", bufs=8))
        outp = ctx.enter_context(tc.tile_pool(name="outs", bufs=12))
        psum = ctx.enter_context(tc.psum_pool(name="psum", bufs=1))
        ctx.enter_context(tc.manual_schedule())

        raw_of = {}
        blk = {}
        state = {"a": 0, "b": 0, "load": 0}

        def load_next():
            if state["load"] >= len(LOADS):
                return
            r0, nb = LOADS[state["load"]]
            if state["load"] == 0:
                t = const.tile([P, nb * E], BF16, name="rawh")
            else:
                t = rawp.tile([P, nb * E], BF16, name="raw%d" % r0)
            state["load"] += 1
            nc.sync.dma_start(out=t[:], in_=xv[:, r0 * E:(r0 + nb) * E])
            for b in range(nb):
                raw_of[r0 + b] = (t, b)

        def psum_bank(kind):
            t = psum.tile([P, 512], F32, tag="%s%d" % (kind, state[kind] % 4), name="p%s%d" % (kind, state[kind]))
            state[kind] += 1
            return t

        ident = const.tile([P, P], F32, name="ident")
        make_identity(nc, ident[:])
        warm = const.tile([P, 1], F32, name="warm")
        nc.vector.memset(warm[:], 0.0)
        nc.scalar.activation(out=warm[:], in_=warm[:], func=TANH)
        bz = const.tile([P, C], BF16, name="bz")
        nc.vector.memset(bz[:], 0.0)
        nc.scalar.dma_start(out=bz[0:1, :], in_=b1)
        coef = const.tile([P, TAPS, P], BF16, name="coef")
        nc.vector.memset(coef[:], 3.0)
        nc.vector.memset(coef[0:1, 0, 0:1], 1.0)
        nc.vector.memset(coef[0:1, 1, 0:1], 2.0)
        shift = const.tile([P, P], F32, name="shift")
        nc.vector.memset(shift[:], 0.0)
        nc.vector.tensor_copy(out=shift[:, 1:P], in_=ident[:, 0:P - 1])

        load_next()
        wraw = const.tile([P, TAPS, 4, C], BF16, name="wraw")
        nc.sync.dma_start(
            out=wraw[:].rearrange("p k (u e) c -> p k u (e c)", u=2),
            in_=W1.rearrange("k (u p e) c -> p k u (e c)", u=2, p=P, e=2),
        )
        for i in range(LEAD):
            load_next()

        wg = const.tile([P, TAPS, C, 4], BF16, name="wg", align_bytes=64)
        wq = const.tile([P, TAPS * C], U32, name="wq", align_bytes=64)
        ws = const.tile([P, TAPS * C], U8, name="ws", align_bytes=64)
        bias = const.tile([P, TAPS, C], F32, name="bias")

        def prepare_w():
            nc.vector.tensor_copy(out=wg[:], in_=wraw[:].rearrange("p k t c -> p k c t"))
            for k in range(TAPS):
                nc.vector.quantize_mx(
                    out=wq[:, k * C:(k + 1) * C].bitcast(FP8X4),
                    scales=ws[:, k * C:(k + 1) * C],
                    in_=wg[:, k].rearrange("p c t -> p (c t)"),
                )

        def transpose_and_leave(u):
            r0, nb = UNITS[u]
            fills = nb // 2
            gs = []
            for first in range(0, fills, 4):
                group = list(range(first, min(first + 4, fills)))
                pas = {}
                for h in group:
                    pa = psum_bank("a")
                    pas[h] = pa
                    for b in range(2):
                        r = r0 + 2 * h + b
                        t, i = raw_of[r % R]
                        words = t[:].bitcast(F32)
                        for v in range(2):
                            lo = i * WORDS + v * P
                            nc.tensor.transpose(
                                pa[:, (2 * b + v) * P:(2 * b + v + 1) * P],
                                words[:, lo:lo + P],
                                (shift if r < 0 else ident)[:],
                            )
                for h in group:
                    if h % 2 == 0:
                        g = grp.tile([P, min(nb, 4) * 2 * P], F32, tag="g", name="g%d_%d" % (u, h), align_bytes=64)
                        gs.append(g)
                    dst = gs[-1][:, (h % 2) * 512:(h % 2 + 1) * 512].rearrange("p (b j v) -> p b j v", b=2, v=2)
                    src = pas[h][:].rearrange("p (b v j) -> p b j v", b=2, v=2)
                    if h in VECTOR_EXITS[fills]:
                        nc.vector.tensor_copy(out=dst, in_=src)
                    else:
                        nc.scalar.copy(out=dst, in_=src)
            return gs

        def quantise(u, n, g):
            r0, nb = UNITS[u]
            w = min(nb, 4)
            cq = qp.tile([P, w * P], U32, tag="cq", name="cq%d_%d" % (u, n), align_bytes=64)
            sq = qp.tile([P, w * P], U8, tag="sq", name="sq%d_%d" % (u, n), align_bytes=64)
            nc.vector.quantize_mx(out=cq[:].bitcast(FP8X4), scales=sq[:], in_=g[:].bitcast(BF16))
            for b in range(w):
                blk[r0 + 4 * n + b] = (cq, sq, b)

        def multiply(u, sizes):
            r0, nb = UNITS[u]
            banks = []
            r = r0
            for n, size in enumerate(sizes):
                pb = psum_bank("b" if n < 4 else "a")
                passes = [(r + h, 0, 2, h) for h in range(0, size, 2)]
                passes += [(r + h - 1, 1, 2, h) for h in range(0, size, 2)]
                for h in range(0, size, 2):
                    passes += [(r + h - 2, 2, 1, h), (r + h + 1, 0, 1, h + 1)]
                for m, (s, k, nk, ob) in enumerate(passes):
                    cq, sq, i = blk[s]
                    nc.tensor.matmul_mx(
                        out=pb[:, ob * C:(ob + nk) * C],
                        lhsT=cq[:, i * P:(i + 1) * P].bitcast(FP8X4),
                        lhsT_scale=sq[:, i * P:(i + 1) * P],
                        rhs=wq[:, k * C:(k + nk) * C].bitcast(FP8X4),
                        rhs_scale=ws[:, k * C:(k + nk) * C],
                        start=(m == 0),
                        stop=(m == len(passes) - 1),
                    )
                banks.append((pb, r, size))
                r += size
            return banks

        o_of = {}

        def add_bias(pb, r, size):
            if r % 8 == 0 or r not in o_of:
                o = outp.tile([P, 8 * C], F32, tag="o", name="o%d" % r)
                for b in range(8):
                    o_of[r + b] = (o, b)
            o, b = o_of[r]
            ob = o[:, b * C:(b + size) * C].rearrange("p (n c) -> p n c", c=C)
            pv = pb[:, 0:size * C].rearrange("p (n c) -> p n c", c=C)
            if r == 0:
                nc.vector.tensor_tensor(out=ob[:, 0:3, :], in0=pv[:, 0:3, :], in1=bias[:], op=ADD)
                nc.vector.tensor_tensor(out=ob[:, 3, :], in0=pv[:, 3, :], in1=bias[:, 2, :], op=ADD)
            else:
                nc.vector.tensor_tensor(out=ob, in0=pv, in1=bias[:, 2:3, :].to_broadcast([P, size, C]), op=ADD)

        def tanh_store(r, size):
            o, b = o_of[r]
            nc.scalar.activation(out=o[:, b * C:(b + size) * C], in_=o[:, b * C:(b + size) * C], func=TANH)
            nc.sync.dma_start(out=ov[:, r * C:(r + size) * C], in_=o[:, b * C:(b + size) * C])

        n_units = len(UNITS)
        for p in range(n_units + 1):
            last = p == n_units
            late = []
            if not last:
                gs = transpose_and_leave(p)
                if p == 0:
                    prepare_w()
                if p == 1:
                    pbias = psum.tile([P, TAPS, C], F32, tag="b3", name="pbias")
                    for k in range(TAPS):
                        nc.tensor.matmul(out=pbias[:, k, :], lhsT=coef[:, k, :], rhs=bz[:], start=True, stop=True)
                for n, g in enumerate(gs):
                    if n == 3:
                        late.append((n, g))
                    else:
                        quantise(p, n, g)
                if p == 1:
                    nc.vector.tensor_copy(out=bias[:], in_=pbias[:])
            banks = []
            if p >= 2:
                nb = UNITS[p - 1][1]
                banks = multiply(p - 1, [4, 4, 4, 2, 2] if last else [4] * (nb // 4))
            if not last:
                for n, (pb, r, size) in enumerate(banks):
                    add_bias(pb, r, size)
                    if n == 0:
                        for m, g in late:
                            quantise(p, m, g)
                        late = []
                for m, g in late:
                    quantise(p, m, g)
            if p >= 3:
                r0, nb = UNITS[p - 2]
                piece = 4 if last else min(nb, 8)
                for r in range(r0, r0 + nb, piece):
                    tanh_store(r, piece)
                    load_next()
            if last:
                for pb, r, size in banks:
                    add_bias(pb, r, size)
                    tanh_store(r, size)
